import numpy as np
import ml_dtypes


def mxq(x, axis, fmt="e4m3"):
    dtype, down = {"e4m3": (ml_dtypes.float8_e4m3fn, 7), "e5m2": (ml_dtypes.float8_e5m2, 14)}[fmt]
    v = np.moveaxis(np.asarray(x, np.float32).astype(ml_dtypes.bfloat16).astype(np.float64), axis, -1)
    blocks = v.reshape(v.shape[:-1] + (-1, 32))
    amax = np.abs(blocks).max(-1, keepdims=True)
    byte = np.maximum(np.where(amax > 0, np.frexp(amax)[1] - 1 + 127, 0) - down, 1)
    scale = np.exp2(byte - 127.0)
    codes = (blocks / scale).astype(np.float32).astype(dtype).astype(np.float64)
    return np.moveaxis((codes * scale).reshape(v.shape), -1, axis)


WIDE = False


def mx_kscale(k):
    if not WIDE:
        return np.ones(k)
    levels = np.array([10, -10, 5, -5, 0])
    if k % 512:
        return np.exp2(np.random.permutation(np.resize(levels, k // 32))).repeat(32)
    a = np.empty((k // 512, 16))
    for p in range(k // 512):
        a[p, :8] = np.random.permutation(np.resize(levels, 8))
        for g in range(8):
            far = levels[np.abs(levels - a[p, g]) >= 10]
            a[p, g + 8] = far[np.random.randint(len(far))]
    return np.exp2(a.ravel()).repeat(32)


BF16 = ml_dtypes.bfloat16


def bf(x):
    return np.asarray(x, np.float32).astype(BF16)


def f64(x):
    return np.asarray(x).astype(np.float64)


B, I, H, P = 512, 1024, 1024, 2048


def sigmoid(v):
    return 1.0 / (1.0 + np.exp(-v))


def setup_inputs():
    s = mx_kscale(H)
    s = s * np.exp2(-np.round(np.log2(s.mean())))
    return {"hidden_new": bf((1.6 + 1.5 * np.random.standard_normal((B, H))) * s),
            "persistent_memory": bf(0.2 * np.random.standard_normal((B, P))),
            "Waddr": bf(np.random.standard_normal((P, H)) * 3.0 / np.sqrt(H) / s[None, :]),
            "baddr": bf(np.random.standard_normal(P)),
            "Wwrite": bf(np.random.standard_normal((P, H)) * 0.7 / np.sqrt(H) / s[None, :]),
            "bwrite": bf(np.random.standard_normal(P)),
            "Wforget": bf(np.random.standard_normal((P, H)) * 0.7 / np.sqrt(H) / s[None, :]),
            "bforget": bf(1.0 + 0.3 * np.random.standard_normal(P))}


def reference(hidden_new, persistent_memory, Waddr, baddr, Wwrite, bwrite, Wforget, bforget):
    hn = f64(hidden_new)
    hq = mxq(hn, 1, "e4m3")
    z = (hq @ mxq(f64(Waddr), 1, "e4m3").T) + f64(baddr)
    e = np.exp(z - z.max(axis=1, keepdims=True))
    addr = e / e.sum(axis=1, keepdims=True)
    write = sigmoid((hq @ mxq(f64(Wwrite), 1, "e4m3").T) + f64(bwrite))
    forget = sigmoid((hq @ mxq(f64(Wforget), 1, "e4m3").T) + f64(bforget))
    hp = np.mean(hn, axis=1, keepdims=True)
    return forget * f64(persistent_memory) + write * hp * addr

@@ -1,0 +1,296 @@
+from contextlib import ExitStack
+
+import concourse.mybir as mybir
+from concourse.masks import make_identity
+
+F32 = mybir.dt.float32
+BF16 = mybir.dt.bfloat16
+U32 = mybir.dt.uint32
+U8 = mybir.dt.uint8
+FP8X4 = mybir.dt.float8_e4m3fn_x4
+ALU = mybir.AluOpType
+ACT = mybir.ActivationFunctionType
+AXIS = mybir.AxisListType
+
+P = 128
+BATCH = 512
+HIDDEN = 1024
+SLOTS = 2048
+PACK = 4
+PASSES = HIDDEN // (P * PACK)
+PAIRS = 2
+ROWS = 512
+ROW_TILES = ROWS // P
+ROW_WORDS = HIDDEN // 2
+BATCH_TILES = BATCH // P
+CHUNKS = SLOTS // ROWS
+SLOT_TILES = SLOTS // P
+RAW_BUFS = 5
+AHEAD = 2
+FORGET = 0
+WRITE = 1
+
+FLOPS = 2 * BATCH * HIDDEN * SLOTS * 3
+
+
+def tile_persistentgrucell_pc_kernel(
+    tc, hidden_new, persistent_memory, Waddr, baddr, Wwrite, bwrite, Wforget, bforget, out
+):
+    nc = tc.nc
+    with ExitStack() as stack:
+        stack.enter_context(tc.manual_schedule())
+        const = stack.enter_context(tc.tile_pool(name="const", bufs=1))
+        raw_pool = stack.enter_context(tc.tile_pool(name="raw", bufs=RAW_BUFS))
+        grouped_pool = stack.enter_context(tc.tile_pool(name="grouped", bufs=2))
+        mx_pool = stack.enter_context(tc.tile_pool(name="mx", bufs=4))
+        score_pool = stack.enter_context(tc.tile_pool(name="score", bufs=2 * BATCH_TILES))
+        gate_pool = stack.enter_context(tc.tile_pool(name="gate", bufs=3))
+        psum = stack.enter_context(tc.psum_pool(name="psum", bufs=8))
+
+        def chunk_rows(weight, c):
+            return weight[c * ROWS : (c + 1) * ROWS, :]
+
+        blocks = []
+        for c in range(CHUNKS):
+            blocks.extend([chunk_rows(Waddr, c), chunk_rows(Wforget, c)])
+        first_write_block = len(blocks)
+        blocks.extend([chunk_rows(Wwrite, c) for c in range(CHUNKS)])
+
+        def load_rows(pool, rows):
+            raw_rows = pool.tile([P, ROW_TILES * HIDDEN], BF16, tag="raw")
+            for j in range(ROW_TILES):
+                nc.sync.dma_start(out=raw_rows[:, j * HIDDEN : (j + 1) * HIDDEN], in_=rows[j * P : (j + 1) * P, :])
+            return raw_rows
+
+        ident = const.tile([P, P], F32)
+        make_identity(nc, ident[:])
+        ident_bf16 = const.tile([P, P], BF16)
+        make_identity(nc, ident_bf16[:])
+        ones = const.tile([P, P], BF16)
+        nc.vector.memset(ones[:], 1.0)
+        bias_rows = const.tile([P, P], BF16)
+        nc.vector.memset(bias_rows[:], 0.0)
+        baddr_row = const.tile([P, SLOTS], BF16)
+        nc.vector.memset(baddr_row[:], 0.0)
+
+        hidden_raw = load_rows(const, hidden_new)
+        raw = {0: load_rows(raw_pool, blocks[0])}
+        for gate, bias in ((FORGET, bforget), (WRITE, bwrite)):
+            nc.sync.dma_start(
+                out=bias_rows[gate * SLOT_TILES : (gate + 1) * SLOT_TILES, :],
+                in_=bias.rearrange("(t p) -> t p", p=P),
+            )
+        nc.sync.dma_start(out=baddr_row[0:1, :], in_=baddr.rearrange("(o n) -> o n", o=1))
+        for n in range(1, AHEAD + 1):
+            raw[n] = load_rows(raw_pool, blocks[n])
+        half_memory = const.tile([P, BATCH_TILES, SLOTS], BF16)
+        nc.sync.dma_start(out=half_memory[:], in_=persistent_memory.rearrange("(i p) n -> p i n", p=P))
+        for n in range(AHEAD + 1, RAW_BUFS):
+            raw[n] = load_rows(raw_pool, blocks[n])
+
+        for c in range(CHUNKS):
+            cols = slice(c * ROWS, (c + 1) * ROWS)
+            nc.gpsimd.tensor_scalar(
+                out=half_memory[:, :, cols], in0=half_memory[:, :, cols], scalar1=0.5, scalar2=0.0, op0=ALU.mult, op1=ALU.add
+            )
+
+        gate_bias = const.tile([P, 2, SLOT_TILES], F32)
+        baddr_all = const.tile([P, SLOTS], BF16)
+
+        def spread_biases():
+            bias_bank = psum.tile([P, P], BF16, tag="bank")
+            nc.tensor.transpose(bias_bank[:], bias_rows[:], ident_bf16[:])
+            nc.scalar.mul(out=gate_bias[:, FORGET, :], in_=bias_bank[:, 0:SLOT_TILES], mul=0.5)
+            nc.scalar.copy(out=gate_bias[:, WRITE, :], in_=bias_bank[:, SLOT_TILES : 2 * SLOT_TILES])
+            for c in range(CHUNKS):
+                cols = slice(c * ROWS, (c + 1) * ROWS)
+                baddr_bank = psum.tile([P, ROWS], F32, tag="bank")
+                nc.tensor.matmul(out=baddr_bank[:], lhsT=ones[:], rhs=baddr_row[:, cols], start=True, stop=True)
+                nc.scalar.copy(out=baddr_all[:, cols], in_=baddr_bank[:])
+
+        def transpose_rows(raw_rows):
+            words = raw_rows[:].bitcast(F32)
+            grouped_rows = grouped_pool.tile([P, PASSES * ROWS * PACK], BF16, tag="grouped", align_bytes=64)
+            grouped_words = grouped_rows[:].bitcast(F32).rearrange("p (g r u) -> p g r u", g=PASSES, u=PAIRS)
+            for j in range(ROW_TILES):
+                bank = psum.tile([P, PASSES * PAIRS, P], F32, tag="bank")
+                for q in range(PASSES * PAIRS):
+                    g, u = divmod(q, PAIRS)
+                    first = j * ROW_WORDS + g * PAIRS * P + u
+                    last = j * ROW_WORDS + (g + 1) * PAIRS * P
+                    nc.tensor.transpose(bank[:, q, :], words[:, first:last:PAIRS], ident[:])
+                nc.scalar.copy(
+                    out=grouped_words[:, :, j * P : (j + 1) * P, :],
+                    in_=bank[:].rearrange("p (g u) r -> p g r u", u=PAIRS),
+                )
+            return grouped_rows
+
+        def quantise(pool, grouped_rows):
+            codes = pool.tile([P, PASSES * ROWS], U32, tag="codes", align_bytes=64)
+            scales = pool.tile([P, PASSES * ROWS], U8, tag="scales", align_bytes=64)
+            nc.vector.quantize_mx(out=codes[:].bitcast(FP8X4), scales=scales[:], in_=grouped_rows[:])
+            return codes, scales
+
+        grouped = {}
+        mx = {}
+
+        def start_block(n):
+            if n < len(blocks):
+                grouped[n] = transpose_rows(raw[n])
+                if n + RAW_BUFS < len(blocks):
+                    raw[n + RAW_BUFS] = load_rows(raw_pool, blocks[n + RAW_BUFS])
+
+        def finish_block(n):
+            if n < len(blocks):
+                mx[n] = quantise(mx_pool, grouped[n])
+
+        def mx_product(acc, stationary, tile_index, moving):
+            for g in range(PASSES):
+                s_cols = slice(g * ROWS + tile_index * P, g * ROWS + (tile_index + 1) * P)
+                m_cols = slice(g * ROWS, (g + 1) * ROWS)
+                nc.tensor.matmul_mx(
+                    out=acc[:],
+                    lhsT=stationary[0][:, s_cols].bitcast(FP8X4),
+                    lhsT_scale=stationary[1][:, s_cols],
+                    rhs=moving[0][:, m_cols].bitcast(FP8X4),
+                    rhs_scale=moving[1][:, m_cols],
+                    start=(g == 0),
+                    stop=(g == PASSES - 1),
+                )
+
+        hidden_sum = const.tile([P, BATCH_TILES], F32)
+        hidden_rows = hidden_raw[:].rearrange("p (i k) -> p i k", i=BATCH_TILES)
+        half = BATCH_TILES // 2
+        nc.vector.tensor_reduce(out=hidden_sum[:, 0:half], in_=hidden_rows[:, 0:half, :], axis=AXIS.X, op=ALU.add)
+        hidden_mx = quantise(const, transpose_rows(hidden_raw))
+        nc.vector.tensor_reduce(
+            out=hidden_sum[:, half:BATCH_TILES], in_=hidden_rows[:, half:BATCH_TILES, :], axis=AXIS.X, op=ALU.add
+        )
+
+        exp_scores = const.tile([P, BATCH_TILES, SLOTS], F32)
+        neg_max = const.tile([P, BATCH_TILES, CHUNKS], F32)
+        exp_sum = const.tile([P, BATCH_TILES, CHUNKS], F32)
+
+        def scores_of(c, addr_mx):
+            cols = slice(c * ROWS, (c + 1) * ROWS)
+            scores = []
+            for i in range(BATCH_TILES):
+                acc = psum.tile([P, ROWS], F32, tag="bank")
+                mx_product(acc, hidden_mx, i, addr_mx)
+                score = score_pool.tile([P, ROWS], F32, tag="score")
+                nc.vector.tensor_tensor(out=score[:], in0=acc[:], in1=baddr_all[:, cols], op=ALU.add)
+                scores.append(score)
+            return scores
+
+        def maxima_of(c, scores):
+            for i in range(BATCH_TILES):
+                nc.vector.tensor_reduce(
+                    out=neg_max[:, i, c : c + 1], in_=scores[i][:], axis=AXIS.X, op=ALU.max, negate=True
+                )
+
+        def exponentials_of(c, scores):
+            cols = slice(c * ROWS, (c + 1) * ROWS)
+            for i in range(BATCH_TILES):
+                nc.scalar.activation(
+                    out=exp_scores[:, i, cols],
+                    in_=scores[i][:],
+                    func=ACT.Exp,
+                    bias=neg_max[:, i, c : c + 1],
+                    scale=1.0,
+                    accum_out=exp_sum[:, i, c : c + 1],
+                )
+
+        def gate_chunk(gate, c, weight_mx, func, scale):
+            gate_t = gate_pool.tile([P, ROW_TILES, BATCH], F32, tag="gate")
+            for j in range(ROW_TILES):
+                acc = psum.tile([P, BATCH], F32, tag="bank")
+                mx_product(acc, weight_mx, j, hidden_mx)
+                t = c * ROW_TILES + j
+                nc.scalar.activation(
+                    out=gate_t[:, j, :], in_=acc[:], func=func, bias=gate_bias[:, gate, t : t + 1], scale=scale
+                )
+            return gate_t
+
+        def batch_rows_of(gate_t, i):
+            bank = psum.tile([P, ROWS], F32, tag="bank")
+            for j in range(ROW_TILES):
+                nc.tensor.transpose(bank[:, j * P : (j + 1) * P], gate_t[:, j, i * P : (i + 1) * P], ident[:])
+            return bank
+
+        result = const.tile([P, BATCH_TILES, SLOTS], F32)
+
+        def keep_memory(c, tanh_t):
+            cols = slice(c * ROWS, (c + 1) * ROWS)
+            for i in range(BATCH_TILES):
+                bank = batch_rows_of(tanh_t, i)
+                nc.vector.scalar_tensor_tensor(
+                    out=result[:, i, cols], in0=bank[:], scalar=1.0, in1=half_memory[:, i, cols], op0=ALU.add, op1=ALU.mult
+                )
+
+        def add_written(c, write_t):
+            cols = slice(c * ROWS, (c + 1) * ROWS)
+            for i in range(BATCH_TILES):
+                bank = batch_rows_of(write_t, i)
+                nc.vector.scalar_tensor_tensor(
+                    out=exp_scores[:, i, cols],
+                    in0=exp_scores[:, i, cols],
+                    scalar=chunk_scale[:, i, c : c + 1],
+                    in1=bank[:],
+                    op0=ALU.mult,
+                    op1=ALU.mult,
+                )
+                adder = (nc.gpsimd, nc.vector)[i % 2]
+                adder.tensor_tensor(
+                    out=result[:, i, cols], in0=result[:, i, cols], in1=exp_scores[:, i, cols], op=ALU.add
+                )
+                nc.sync.dma_start(out=out[i * P : (i + 1) * P, cols], in_=result[:, i, cols])
+
+        start_block(0)
+        finish_block(0)
+        spread_biases()
+        start_block(1)
+        finish_block(1)
+
+        for c in range(CHUNKS):
+            addr_block = 2 * c
+            forget_block = addr_block + 1
+            scores = scores_of(c, mx[addr_block])
+            start_block(addr_block + AHEAD)
+            maxima_of(c, scores)
+            finish_block(addr_block + AHEAD)
+            tanh_t = gate_chunk(FORGET, c, mx[forget_block], ACT.Tanh, 0.5)
+            start_block(forget_block + AHEAD)
+            exponentials_of(c, scores)
+            keep_memory(c, tanh_t)
+            finish_block(forget_block + AHEAD)
+
+        small = [P, BATCH_TILES, CHUNKS]
+        neg_top = const.tile([P, BATCH_TILES], F32)
+        nc.vector.tensor_reduce(out=neg_top[:], in_=neg_max[:], axis=AXIS.X, op=ALU.min)
+        below_top = const.tile(small, F32)
+        nc.vector.tensor_tensor(
+            out=below_top[:], in0=neg_top[:].unsqueeze(2).to_broadcast(small), in1=neg_max[:], op=ALU.subtract
+        )
+        rescale = const.tile(small, F32)
+        nc.scalar.activation(out=rescale[:], in_=below_top[:], func=ACT.Exp)
+        rescaled_sum = const.tile(small, F32)
+        nc.vector.tensor_tensor(out=rescaled_sum[:], in0=rescale[:], in1=exp_sum[:], op=ALU.mult)
+        row_sum = const.tile([P, BATCH_TILES], F32)
+        nc.vector.tensor_reduce(out=row_sum[:], in_=rescaled_sum[:], axis=AXIS.X, op=ALU.add)
+        inv_row_sum = const.tile([P, BATCH_TILES], F32)
+        nc.vector.reciprocal(out=inv_row_sum[:], in_=row_sum[:])
+        row_scale = const.tile([P, BATCH_TILES], F32)
+        nc.vector.scalar_tensor_tensor(
+            out=row_scale[:], in0=hidden_sum[:], scalar=1.0 / HIDDEN, in1=inv_row_sum[:], op0=ALU.mult, op1=ALU.mult
+        )
+        chunk_scale = const.tile(small, F32)
+        nc.vector.tensor_tensor(
+            out=chunk_scale[:], in0=rescale[:], in1=row_scale[:].unsqueeze(2).to_broadcast(small), op=ALU.mult
+        )
+
+        for c in range(CHUNKS):
+            write_block = first_write_block + c
+            write_t = gate_chunk(WRITE, c, mx[write_block], ACT.Sigmoid, 1.0)
+            start_block(write_block + AHEAD)
+            add_written(c, write_t)
+            finish_block(write_block + AHEAD)

@@ -20,16 +20,23 @@ PACK = 4
 PASSES = HIDDEN // (P * PACK)
 PAIRS = 2
 ROWS = 512
-ROW_TILES = ROWS // P
+TILES = ROWS // P
 ROW_WORDS = HIDDEN // 2
-BATCH_TILES = BATCH // P
 CHUNKS = SLOTS // ROWS
 SLOT_TILES = SLOTS // P
 RAW_BUFS = 5
 AHEAD = 2
-FORGET = 0
-WRITE = 1
+ADDR = 0
+FORGET = 1
+WRITE = 2
+ORDER = (
+    (ADDR, 0), (FORGET, 0), (ADDR, 1), (FORGET, 1), (ADDR, 2), (FORGET, 2), (ADDR, 3), (FORGET, 3), (WRITE, 0), (WRITE, 1), (WRITE, 2), (WRITE, 3),
+)
 
+SCALED = {(c, i) for c in (1, 2, 3) for i in (0, 1)}
+ON_GPSIMD = SCALED
+PERMUTE = "------------"
+GP_ADDS = "1111111111111010"
 FLOPS = 2 * BATCH * HIDDEN * SLOTS * 3
 
 
@@ -43,23 +50,21 @@ def tile_persistentgrucell_pc_kernel(
         raw_pool = stack.enter_context(tc.tile_pool(name="raw", bufs=RAW_BUFS))
         grouped_pool = stack.enter_context(tc.tile_pool(name="grouped", bufs=2))
         mx_pool = stack.enter_context(tc.tile_pool(name="mx", bufs=4))
-        score_pool = stack.enter_context(tc.tile_pool(name="score", bufs=2 * BATCH_TILES))
-        gate_pool = stack.enter_context(tc.tile_pool(name="gate", bufs=3))
+        lined_pool = stack.enter_context(tc.tile_pool(name="lined", bufs=2))
+        score_pool = stack.enter_context(tc.tile_pool(name="score", bufs=2 * TILES))
+        gate_pool = stack.enter_context(tc.tile_pool(name="gate", bufs=2))
         psum = stack.enter_context(tc.psum_pool(name="psum", bufs=8))
 
-        def chunk_rows(weight, c):
-            return weight[c * ROWS : (c + 1) * ROWS, :]
+        weights = {ADDR: Waddr, FORGET: Wforget, WRITE: Wwrite}
+        blocks = [weights[kind][c * ROWS : (c + 1) * ROWS, :] for kind, c in ORDER]
 
-        blocks = []
-        for c in range(CHUNKS):
-            blocks.extend([chunk_rows(Waddr, c), chunk_rows(Wforget, c)])
-        first_write_block = len(blocks)
-        blocks.extend([chunk_rows(Wwrite, c) for c in range(CHUNKS)])
-
-        def load_rows(pool, rows):
-            raw_rows = pool.tile([P, ROW_TILES * HIDDEN], BF16, tag="raw")
-            for j in range(ROW_TILES):
-                nc.sync.dma_start(out=raw_rows[:, j * HIDDEN : (j + 1) * HIDDEN], in_=rows[j * P : (j + 1) * P, :])
+        def load_rows(pool, rows, pieces):
+            raw_rows = pool.tile([P, TILES * HIDDEN], BF16, tag="raw")
+            tiles = raw_rows[:].rearrange("p (j k) -> p j k", j=TILES)
+            source = rows.rearrange("(j p) k -> p j k", p=P)
+            step = TILES // pieces
+            for j in range(0, TILES, step):
+                nc.sync.dma_start(out=tiles[:, j : j + step, :], in_=source[:, j : j + step, :])
             return raw_rows
 
         ident = const.tile([P, P], F32)
@@ -67,230 +72,333 @@ def tile_persistentgrucell_pc_kernel(
         ident_bf16 = const.tile([P, P], BF16)
         make_identity(nc, ident_bf16[:])
         ones = const.tile([P, P], BF16)
-        nc.vector.memset(ones[:], 1.0)
         bias_rows = const.tile([P, P], BF16)
         nc.vector.memset(bias_rows[:], 0.0)
         baddr_row = const.tile([P, SLOTS], BF16)
         nc.vector.memset(baddr_row[:], 0.0)
+        nc.vector.memset(ones[:], 1.0)
 
-        hidden_raw = load_rows(const, hidden_new)
-        raw = {0: load_rows(raw_pool, blocks[0])}
-        for gate, bias in ((FORGET, bforget), (WRITE, bwrite)):
+        hidden_raw = load_rows(const, hidden_new, 2)
+        raw = {0: load_rows(raw_pool, blocks[0], 2)}
+        for gate, bias in ((0, bforget), (1, bwrite)):
             nc.sync.dma_start(
                 out=bias_rows[gate * SLOT_TILES : (gate + 1) * SLOT_TILES, :],
                 in_=bias.rearrange("(t p) -> t p", p=P),
             )
         nc.sync.dma_start(out=baddr_row[0:1, :], in_=baddr.rearrange("(o n) -> o n", o=1))
-        for n in range(1, AHEAD + 1):
-            raw[n] = load_rows(raw_pool, blocks[n])
-        half_memory = const.tile([P, BATCH_TILES, SLOTS], BF16)
+        raw[1] = load_rows(raw_pool, blocks[1], 2)
+        raw[2] = load_rows(raw_pool, blocks[2], 2)
+        half_memory = const.tile([P, TILES, SLOTS], BF16)
         nc.sync.dma_start(out=half_memory[:], in_=persistent_memory.rearrange("(i p) n -> p i n", p=P))
-        for n in range(AHEAD + 1, RAW_BUFS):
-            raw[n] = load_rows(raw_pool, blocks[n])
+        for n in range(3, RAW_BUFS):
+            raw[n] = load_rows(raw_pool, blocks[n], 2)
 
-        for c in range(CHUNKS):
-            cols = slice(c * ROWS, (c + 1) * ROWS)
-            nc.gpsimd.tensor_scalar(
-                out=half_memory[:, :, cols], in0=half_memory[:, :, cols], scalar1=0.5, scalar2=0.0, op0=ALU.mult, op1=ALU.add
-            )
-
-        gate_bias = const.tile([P, 2, SLOT_TILES], F32)
+        gate_bias = const.tile([P, 2 * SLOT_TILES], F32)
         baddr_all = const.tile([P, SLOTS], BF16)
 
-        def spread_biases():
+        def spread_gate_biases():
             bias_bank = psum.tile([P, P], BF16, tag="bank")
             nc.tensor.transpose(bias_bank[:], bias_rows[:], ident_bf16[:])
-            nc.scalar.mul(out=gate_bias[:, FORGET, :], in_=bias_bank[:, 0:SLOT_TILES], mul=0.5)
-            nc.scalar.copy(out=gate_bias[:, WRITE, :], in_=bias_bank[:, SLOT_TILES : 2 * SLOT_TILES])
+            nc.scalar.mul(out=gate_bias[:], in_=bias_bank[:, 0 : 2 * SLOT_TILES], mul=0.5)
+
+        def spread_baddr():
             for c in range(CHUNKS):
                 cols = slice(c * ROWS, (c + 1) * ROWS)
                 baddr_bank = psum.tile([P, ROWS], F32, tag="bank")
                 nc.tensor.matmul(out=baddr_bank[:], lhsT=ones[:], rhs=baddr_row[:, cols], start=True, stop=True)
                 nc.scalar.copy(out=baddr_all[:, cols], in_=baddr_bank[:])
 
-        def transpose_rows(raw_rows):
-            words = raw_rows[:].bitcast(F32)
-            grouped_rows = grouped_pool.tile([P, PASSES * ROWS * PACK], BF16, tag="grouped", align_bytes=64)
-            grouped_words = grouped_rows[:].bitcast(F32).rearrange("p (g r u) -> p g r u", g=PASSES, u=PAIRS)
-            for j in range(ROW_TILES):
-                bank = psum.tile([P, PASSES * PAIRS, P], F32, tag="bank")
-                for q in range(PASSES * PAIRS):
-                    g, u = divmod(q, PAIRS)
-                    first = j * ROW_WORDS + g * PAIRS * P + u
-                    last = j * ROW_WORDS + (g + 1) * PAIRS * P
-                    nc.tensor.transpose(bank[:, q, :], words[:, first:last:PAIRS], ident[:])
-                nc.scalar.copy(
-                    out=grouped_words[:, :, j * P : (j + 1) * P, :],
-                    in_=bank[:].rearrange("p (g u) r -> p g r u", u=PAIRS),
-                )
-            return grouped_rows
-
-        def quantise(pool, grouped_rows):
-            codes = pool.tile([P, PASSES * ROWS], U32, tag="codes", align_bytes=64)
-            scales = pool.tile([P, PASSES * ROWS], U8, tag="scales", align_bytes=64)
-            nc.vector.quantize_mx(out=codes[:].bitcast(FP8X4), scales=scales[:], in_=grouped_rows[:])
-            return codes, scales
-
         grouped = {}
         mx = {}
+        lined = {}
 
-        def start_block(n):
-            if n < len(blocks):
-                grouped[n] = transpose_rows(raw[n])
-                if n + RAW_BUFS < len(blocks):
-                    raw[n + RAW_BUFS] = load_rows(raw_pool, blocks[n + RAW_BUFS])
+        def line_up(n):
+            if n >= len(blocks) or PERMUTE[n] == "-":
+                return
+            lined_rows = lined_pool.tile([P, TILES * HIDDEN], BF16, tag="lined")
+            lined[n] = lined_rows
+            source = raw[n][:].bitcast(F32).rearrange("p (b u i) -> p u b i", u=PAIRS, i=8)
+            target = lined[n][:].bitcast(F32).rearrange("p (u b i) -> p u b i", u=PAIRS, i=8)
+            if PERMUTE[n] == "V":
+                nc.vector.tensor_copy(out=target, in_=source)
+            else:
+                nc.scalar.copy(out=target, in_=source)
+            load_later(n)
 
-        def finish_block(n):
-            if n < len(blocks):
-                mx[n] = quantise(mx_pool, grouped[n])
+        def stationary(n):
+            return n != "hidden" and ORDER[n][0] != ADDR
 
-        def mx_product(acc, stationary, tile_index, moving):
+        def grouped_view(n, j):
+            words = grouped[n][:].bitcast(F32)
+            if stationary(n):
+                return words.rearrange("p (j g r u) -> p j g r u", j=TILES, g=PASSES, u=PAIRS)[:, j]
+            return words.rearrange("p (g j r u) -> p j g r u", j=TILES, g=PASSES, u=PAIRS)[:, j]
+
+        def transpose_tiles(n, raw_rows, tiles):
+            words = lined[n][:].bitcast(F32) if n in lined else raw_rows[:].bitcast(F32)
+            if n not in grouped:
+                grouped_rows = grouped_pool.tile([P, PASSES * ROWS * PACK], BF16, tag="grouped", align_bytes=64)
+                grouped[n] = grouped_rows
+            banks = []
+            for j in tiles:
+                bank = psum.tile([P, PASSES, PAIRS, P], F32, tag="bank")
+                for g in range(PASSES):
+                    for u in range(PAIRS):
+                        if n in lined:
+                            first = ((u * TILES + j) * PASSES + g) * P
+                            columns = slice(first, first + P)
+                        else:
+                            first = j * ROW_WORDS + g * PAIRS * P + u
+                            columns = slice(first, j * ROW_WORDS + (g + 1) * PAIRS * P, PAIRS)
+                        nc.tensor.transpose(bank[:, g, u, :], words[:, columns], ident[:])
+                banks.append(bank)
+            for j, bank in zip(tiles, banks):
+                nc.scalar.copy(out=grouped_view(n, j), in_=bank[:].rearrange("p g u r -> p g r u"))
+
+        def quantise(n, pool, first, last):
+            if n not in mx:
+                new_codes = pool.tile([P, PASSES * ROWS], U32, tag="codes", align_bytes=64)
+                new_scales = pool.tile([P, PASSES * ROWS], U8, tag="scales", align_bytes=64)
+                mx[n] = (new_codes, new_scales)
+            codes, scales = mx[n]
+            a, b = first * PASSES * P, last * PASSES * P
+            nc.vector.quantize_mx(
+                out=codes[:, a:b].bitcast(FP8X4), scales=scales[:, a:b], in_=grouped[n][:, a * PACK : b * PACK]
+            )
+
+        def mx_product(acc, still, still_cols, moving):
             for g in range(PASSES):
-                s_cols = slice(g * ROWS + tile_index * P, g * ROWS + (tile_index + 1) * P)
+                s_cols = still_cols(g)
                 m_cols = slice(g * ROWS, (g + 1) * ROWS)
                 nc.tensor.matmul_mx(
                     out=acc[:],
-                    lhsT=stationary[0][:, s_cols].bitcast(FP8X4),
-                    lhsT_scale=stationary[1][:, s_cols],
+                    lhsT=still[0][:, s_cols].bitcast(FP8X4),
+                    lhsT_scale=still[1][:, s_cols],
                     rhs=moving[0][:, m_cols].bitcast(FP8X4),
                     rhs_scale=moving[1][:, m_cols],
                     start=(g == 0),
                     stop=(g == PASSES - 1),
                 )
 
-        hidden_sum = const.tile([P, BATCH_TILES], F32)
-        hidden_rows = hidden_raw[:].rearrange("p (i k) -> p i k", i=BATCH_TILES)
-        half = BATCH_TILES // 2
-        nc.vector.tensor_reduce(out=hidden_sum[:, 0:half], in_=hidden_rows[:, 0:half, :], axis=AXIS.X, op=ALU.add)
-        hidden_mx = quantise(const, transpose_rows(hidden_raw))
-        nc.vector.tensor_reduce(
-            out=hidden_sum[:, half:BATCH_TILES], in_=hidden_rows[:, half:BATCH_TILES, :], axis=AXIS.X, op=ALU.add
-        )
+        exp_scores = const.tile([P, TILES, SLOTS], F32)
+        neg_max = const.tile([P, TILES, CHUNKS], F32)
+        exp_sum = const.tile([P, TILES, CHUNKS], F32)
+        result = const.tile([P, TILES, SLOTS], F32)
+        scores = {}
+        gates = {}
 
-        exp_scores = const.tile([P, BATCH_TILES, SLOTS], F32)
-        neg_max = const.tile([P, BATCH_TILES, CHUNKS], F32)
-        exp_sum = const.tile([P, BATCH_TILES, CHUNKS], F32)
+        def score(n, i):
+            c = ORDER[n][1]
+            acc = psum.tile([P, ROWS], F32, tag="bank")
+            mx_product(acc, mx["hidden"], lambda g: slice(g * ROWS + i * P, g * ROWS + (i + 1) * P), mx[n])
+            z = score_pool.tile([P, ROWS], F32, tag="score")
+            nc.vector.tensor_tensor(out=z[:], in0=acc[:], in1=baddr_all[:, c * ROWS : (c + 1) * ROWS], op=ALU.add)
+            scores[n, i] = z
 
-        def scores_of(c, addr_mx):
+        def maximum(n, i):
+            c = ORDER[n][1]
+            nc.vector.tensor_reduce(out=neg_max[:, i, c : c + 1], in_=scores[n, i][:], axis=AXIS.X, op=ALU.max, negate=True)
+
+        def exponential(n, i):
+            c = ORDER[n][1]
+            nc.scalar.activation(
+                out=exp_scores[:, i, c * ROWS : (c + 1) * ROWS], in_=scores[n, i][:], func=ACT.Exp,
+                bias=neg_max[:, i, c : c + 1], scale=1.0, accum_out=exp_sum[:, i, c : c + 1],
+            )
+
+        def gate(n, j):
+            kind, c = ORDER[n]
+            acc = psum.tile([P, BATCH], F32, tag="bank")
+            mx_product(acc, mx[n], lambda g: slice((j * PASSES + g) * P, (j * PASSES + g + 1) * P), mx["hidden"])
+            if n not in gates:
+                gate_t = gate_pool.tile([P, TILES, BATCH], F32, tag="gate")
+                gates[n] = gate_t
+            t = (kind - FORGET) * SLOT_TILES + c * TILES + j
+            nc.scalar.activation(
+                out=gates[n][:, j, :],
+                in_=acc[:],
+                func=ACT.Tanh,
+                bias=gate_bias[:, t : t + 1],
+                scale=0.5,
+            )
+
+        def product(n, i):
+            if ORDER[n][0] == ADDR:
+                score(n, i)
+            else:
+                gate(n, i)
+
+        def turn_back(n):
+            kind, c = ORDER[n]
             cols = slice(c * ROWS, (c + 1) * ROWS)
-            scores = []
-            for i in range(BATCH_TILES):
-                acc = psum.tile([P, ROWS], F32, tag="bank")
-                mx_product(acc, hidden_mx, i, addr_mx)
-                score = score_pool.tile([P, ROWS], F32, tag="score")
-                nc.vector.tensor_tensor(out=score[:], in0=acc[:], in1=baddr_all[:, cols], op=ALU.add)
-                scores.append(score)
-            return scores
+            banks = []
+            for i in range(TILES):
+                bank = psum.tile([P, ROWS], F32, tag="bank")
+                for j in range(TILES):
+                    nc.tensor.transpose(bank[:, j * P : (j + 1) * P], gates[n][:, j, i * P : (i + 1) * P], ident[:])
+                banks.append(bank)
+            return banks
 
-        def maxima_of(c, scores):
-            for i in range(BATCH_TILES):
-                nc.vector.tensor_reduce(
-                    out=neg_max[:, i, c : c + 1], in_=scores[i][:], axis=AXIS.X, op=ALU.max, negate=True
-                )
-
-        def exponentials_of(c, scores):
+        def multiply(n, i, bank):
+            kind, c = ORDER[n]
             cols = slice(c * ROWS, (c + 1) * ROWS)
-            for i in range(BATCH_TILES):
-                nc.scalar.activation(
-                    out=exp_scores[:, i, cols],
-                    in_=scores[i][:],
-                    func=ACT.Exp,
-                    bias=neg_max[:, i, c : c + 1],
-                    scale=1.0,
-                    accum_out=exp_sum[:, i, c : c + 1],
-                )
-
-        def gate_chunk(gate, c, weight_mx, func, scale):
-            gate_t = gate_pool.tile([P, ROW_TILES, BATCH], F32, tag="gate")
-            for j in range(ROW_TILES):
-                acc = psum.tile([P, BATCH], F32, tag="bank")
-                mx_product(acc, weight_mx, j, hidden_mx)
-                t = c * ROW_TILES + j
-                nc.scalar.activation(
-                    out=gate_t[:, j, :], in_=acc[:], func=func, bias=gate_bias[:, gate, t : t + 1], scale=scale
-                )
-            return gate_t
-
-        def batch_rows_of(gate_t, i):
-            bank = psum.tile([P, ROWS], F32, tag="bank")
-            for j in range(ROW_TILES):
-                nc.tensor.transpose(bank[:, j * P : (j + 1) * P], gate_t[:, j, i * P : (i + 1) * P], ident[:])
-            return bank
-
-        result = const.tile([P, BATCH_TILES, SLOTS], F32)
-
-        def keep_memory(c, tanh_t):
-            cols = slice(c * ROWS, (c + 1) * ROWS)
-            for i in range(BATCH_TILES):
-                bank = batch_rows_of(tanh_t, i)
+            if kind == FORGET:
                 nc.vector.scalar_tensor_tensor(
                     out=result[:, i, cols], in0=bank[:], scalar=1.0, in1=half_memory[:, i, cols], op0=ALU.add, op1=ALU.mult
                 )
-
-        def add_written(c, write_t):
-            cols = slice(c * ROWS, (c + 1) * ROWS)
-            for i in range(BATCH_TILES):
-                bank = batch_rows_of(write_t, i)
+            else:
                 nc.vector.scalar_tensor_tensor(
-                    out=exp_scores[:, i, cols],
-                    in0=exp_scores[:, i, cols],
-                    scalar=chunk_scale[:, i, c : c + 1],
-                    in1=bank[:],
-                    op0=ALU.mult,
-                    op1=ALU.mult,
+                    out=exp_scores[:, i, cols], in0=bank[:], scalar=1.0, in1=exp_scores[:, i, cols], op0=ALU.add, op1=ALU.mult
                 )
-                adder = (nc.gpsimd, nc.vector)[i % 2]
-                adder.tensor_tensor(
-                    out=result[:, i, cols], in0=result[:, i, cols], in1=exp_scores[:, i, cols], op=ALU.add
-                )
-                nc.sync.dma_start(out=out[i * P : (i + 1) * P, cols], in_=result[:, i, cols])
 
-        start_block(0)
-        finish_block(0)
-        spread_biases()
-        start_block(1)
-        finish_block(1)
-
-        for c in range(CHUNKS):
-            addr_block = 2 * c
-            forget_block = addr_block + 1
-            scores = scores_of(c, mx[addr_block])
-            start_block(addr_block + AHEAD)
-            maxima_of(c, scores)
-            finish_block(addr_block + AHEAD)
-            tanh_t = gate_chunk(FORGET, c, mx[forget_block], ACT.Tanh, 0.5)
-            start_block(forget_block + AHEAD)
-            exponentials_of(c, scores)
-            keep_memory(c, tanh_t)
-            finish_block(forget_block + AHEAD)
-
-        small = [P, BATCH_TILES, CHUNKS]
-        neg_top = const.tile([P, BATCH_TILES], F32)
-        nc.vector.tensor_reduce(out=neg_top[:], in_=neg_max[:], axis=AXIS.X, op=ALU.min)
-        below_top = const.tile(small, F32)
-        nc.vector.tensor_tensor(
-            out=below_top[:], in0=neg_top[:].unsqueeze(2).to_broadcast(small), in1=neg_max[:], op=ALU.subtract
-        )
-        rescale = const.tile(small, F32)
-        nc.scalar.activation(out=rescale[:], in_=below_top[:], func=ACT.Exp)
-        rescaled_sum = const.tile(small, F32)
-        nc.vector.tensor_tensor(out=rescaled_sum[:], in0=rescale[:], in1=exp_sum[:], op=ALU.mult)
-        row_sum = const.tile([P, BATCH_TILES], F32)
-        nc.vector.tensor_reduce(out=row_sum[:], in_=rescaled_sum[:], axis=AXIS.X, op=ALU.add)
-        inv_row_sum = const.tile([P, BATCH_TILES], F32)
-        nc.vector.reciprocal(out=inv_row_sum[:], in_=row_sum[:])
-        row_scale = const.tile([P, BATCH_TILES], F32)
-        nc.vector.scalar_tensor_tensor(
-            out=row_scale[:], in0=hidden_sum[:], scalar=1.0 / HIDDEN, in1=inv_row_sum[:], op0=ALU.mult, op1=ALU.mult
-        )
+        small = [P, TILES, CHUNKS]
         chunk_scale = const.tile(small, F32)
-        nc.vector.tensor_tensor(
-            out=chunk_scale[:], in0=rescale[:], in1=row_scale[:].unsqueeze(2).to_broadcast(small), op=ALU.mult
-        )
+        hidden_sum = const.tile([P, TILES], F32)
+        neg_top = const.tile([P, TILES], F32)
+        below_top = const.tile(small, F32)
+        rescale = const.tile(small, F32)
+        rescaled_sum = const.tile(small, F32)
+        row_sum = const.tile([P, TILES], F32)
+        inv_row_sum = const.tile([P, TILES], F32)
+        row_scale = const.tile([P, TILES], F32)
 
-        for c in range(CHUNKS):
-            write_block = first_write_block + c
-            write_t = gate_chunk(WRITE, c, mx[write_block], ACT.Sigmoid, 1.0)
-            start_block(write_block + AHEAD)
-            add_written(c, write_t)
-            finish_block(write_block + AHEAD)
+        totals = [
+            lambda: nc.vector.tensor_reduce(out=neg_top[:], in_=neg_max[:], axis=AXIS.X, op=ALU.min),
+            lambda: nc.vector.tensor_tensor(
+                out=below_top[:], in0=neg_top[:].unsqueeze(2).to_broadcast(small), in1=neg_max[:], op=ALU.subtract
+            ),
+            lambda: nc.scalar.activation(out=rescale[:], in_=below_top[:], func=ACT.Exp),
+            lambda: nc.vector.tensor_tensor(out=rescaled_sum[:], in0=rescale[:], in1=exp_sum[:], op=ALU.mult),
+            lambda: nc.vector.tensor_reduce(out=row_sum[:], in_=rescaled_sum[:], axis=AXIS.X, op=ALU.add),
+            lambda: nc.vector.reciprocal(out=inv_row_sum[:], in_=row_sum[:]),
+            lambda: nc.vector.scalar_tensor_tensor(
+                out=row_scale[:], in0=hidden_sum[:], scalar=0.5 / HIDDEN, in1=inv_row_sum[:], op0=ALU.mult, op1=ALU.mult
+            ),
+            lambda: nc.vector.tensor_tensor(
+                out=chunk_scale[:], in0=rescale[:], in1=row_scale[:].unsqueeze(2).to_broadcast(small), op=ALU.mult
+            ),
+        ]
+
+        def scale_scores(c):
+            for i in range(TILES):
+                if (c, i) in SCALED:
+                    cols = slice(c * ROWS, (c + 1) * ROWS)
+                    nc.scalar.mul(out=exp_scores[:, i, cols], in_=exp_scores[:, i, cols], mul=chunk_scale[:, i, c : c + 1])
+
+        def finish(c, i):
+            cols = slice(c * ROWS, (c + 1) * ROWS)
+            if (c, i) in SCALED:
+                adder = nc.gpsimd if (c, i) in ON_GPSIMD else nc.vector
+                adder.tensor_tensor(
+                    out=result[:, i, cols], in0=exp_scores[:, i, cols], in1=result[:, i, cols], op=ALU.add
+                )
+            else:
+                nc.vector.scalar_tensor_tensor(
+                    out=result[:, i, cols], in0=exp_scores[:, i, cols], scalar=chunk_scale[:, i, c : c + 1],
+                    in1=result[:, i, cols], op0=ALU.mult, op1=ALU.add,
+                )
+            nc.sync.dma_start(out=out[i * P : (i + 1) * P, cols], in_=result[:, i, cols])
+
+        def load_later(n):
+            if n + RAW_BUFS < len(blocks):
+                raw[n + RAW_BUFS] = load_rows(raw_pool, blocks[n + RAW_BUFS], 2)
+
+        half = TILES // 2
+        hidden_rows = hidden_raw[:].rearrange("p (i k) -> p i k", i=TILES)
+
+        def sum_hidden(first, last):
+            nc.vector.tensor_reduce(
+                out=hidden_sum[:, first:last], in_=hidden_rows[:, first:last, :], axis=AXIS.X, op=ALU.add
+            )
+
+        def halve_memory(c):
+            cols = slice(c * ROWS, (c + 1) * ROWS)
+            nc.vector.tensor_scalar(
+                out=half_memory[:, :, cols], in0=half_memory[:, :, cols], scalar1=0.5, scalar2=None, op0=ALU.mult
+            )
+
+        count = len(ORDER)
+        last_addr = max(n for n in range(count) if ORDER[n][0] == ADDR)
+
+        def is_addr(n):
+            return 0 <= n < count and ORDER[n][0] == ADDR
+
+        def start_block(n):
+            if n < count:
+                transpose_tiles(n, raw[n], (0, 1))
+                transpose_tiles(n, raw[n], (2, 3))
+                if n not in lined:
+                    load_later(n)
+
+        def finish_block(n):
+            if n < count:
+                quantise(n, mx_pool, 0, TILES)
+
+        sum_hidden(0, half)
+        transpose_tiles("hidden", hidden_raw, (0, 1))
+        transpose_tiles("hidden", hidden_raw, (2, 3))
+        quantise("hidden", const, 0, TILES)
+
+        def begin_and_finish(n):
+            if n < count and stationary(n):
+                transpose_tiles(n, raw[n], (0, 1))
+                quantise(n, mx_pool, 0, half)
+                transpose_tiles(n, raw[n], (2, 3))
+                quantise(n, mx_pool, half, TILES)
+                load_later(n)
+            else:
+                start_block(n)
+                finish_block(n)
+
+        begin_and_finish(0)
+        spread_gate_biases()
+        sum_hidden(half, TILES)
+        if is_addr(0):
+            spread_baddr()
+            begin_and_finish(1)
+        left = {}
+        ready = []
+        exps = []
+        for n in range(count):
+            kind, c = ORDER[n]
+            for i in range(TILES):
+                product(n, i)
+            if n == 0 and not is_addr(0):
+                start_block(1)
+                finish_block(1)
+                spread_baddr()
+            start_block(n + 2)
+            if is_addr(n):
+                for i in range(TILES):
+                    maximum(n, i)
+                exps.append(n)
+                if kind == ADDR and n == last_addr:
+                    totals[0]()
+                    totals[1]()
+            if (not is_addr(n) or n + 1 < count and is_addr(n + 1)) and exps and exps[0] < n:
+                m = exps.pop(0)
+                for i in range(TILES):
+                    exponential(m, i)
+                if m == last_addr:
+                    totals[2]()
+            if not is_addr(n):
+                if kind == FORGET:
+                    halve_memory(c)
+                banks = turn_back(n)
+                for i in range(TILES):
+                    multiply(n, i, banks[i])
+                left[c] = left.get(c, 0) + 1
+                if left[c] == 2:
+                    ready.append(c)
+            finish_block(n + 2)
+            if n == last_addr + 1:
+                for step in totals[3:]:
+                    step()
+            if n > last_addr and n + 1 < count and ORDER[n + 1][0] == WRITE:
+                scale_scores(ORDER[n + 1][1])
+            if n > last_addr:
+                for k in range(1 if n + 1 < count else len(ready)):
+                    if ready:
+                        c = ready.pop(0)
+                        for i in range(TILES):
+                            finish(c, i)

@@ -33,8 +33,9 @@ ORDER = (
     (ADDR, 0), (FORGET, 0), (ADDR, 1), (FORGET, 1), (ADDR, 2), (FORGET, 2), (ADDR, 3), (FORGET, 3), (WRITE, 0), (WRITE, 1), (WRITE, 2), (WRITE, 3),
 )
 
-SCALED = {(c, i) for c in (1, 2, 3) for i in (0, 1)}
+SCALED = {(1, 0), (2, 0), (3, 0)}
 ON_GPSIMD = SCALED
+MAX_WIDE = 4
 PERMUTE = "------------"
 GP_ADDS = "1111111111111010"
 FLOPS = 2 * BATCH * HIDDEN * SLOTS * 3
@@ -51,7 +52,7 @@ def tile_persistentgrucell_pc_kernel(
         grouped_pool = stack.enter_context(tc.tile_pool(name="grouped", bufs=2))
         mx_pool = stack.enter_context(tc.tile_pool(name="mx", bufs=4))
         lined_pool = stack.enter_context(tc.tile_pool(name="lined", bufs=2))
-        score_pool = stack.enter_context(tc.tile_pool(name="score", bufs=2 * TILES))
+        score_pool = stack.enter_context(tc.tile_pool(name="score", bufs=2))
         gate_pool = stack.enter_context(tc.tile_pool(name="gate", bufs=2))
         psum = stack.enter_context(tc.psum_pool(name="psum", bufs=8))
 
@@ -86,11 +87,21 @@ def tile_persistentgrucell_pc_kernel(
                 in_=bias.rearrange("(t p) -> t p", p=P),
             )
         nc.sync.dma_start(out=baddr_row[0:1, :], in_=baddr.rearrange("(o n) -> o n", o=1))
-        raw[1] = load_rows(raw_pool, blocks[1], 2)
-        raw[2] = load_rows(raw_pool, blocks[2], 2)
         half_memory = const.tile([P, TILES, SLOTS], BF16)
-        nc.sync.dma_start(out=half_memory[:], in_=persistent_memory.rearrange("(i p) n -> p i n", p=P))
-        for n in range(3, RAW_BUFS):
+        memory = persistent_memory.rearrange("(i p) n -> p i n", p=P)
+
+        def load_memory(c):
+            cols = slice(c * ROWS, (c + 1) * ROWS)
+            nc.sync.dma_start(out=half_memory[:, :, cols], in_=memory[:, :, cols])
+            for i in range(TILES):
+                nc.gpsimd.tensor_scalar(
+                    out=half_memory[:, i, cols], in0=half_memory[:, i, cols], scalar1=0.5, scalar2=0.0, op0=ALU.mult, op1=ALU.add
+                )
+
+        for n in range(1, 4):
+            raw[n] = load_rows(raw_pool, blocks[n], 2)
+        load_memory(0)
+        for n in range(4, RAW_BUFS):
             raw[n] = load_rows(raw_pool, blocks[n], 2)
 
         gate_bias = const.tile([P, 2 * SLOT_TILES], F32)
@@ -191,18 +202,24 @@ def tile_persistentgrucell_pc_kernel(
             c = ORDER[n][1]
             acc = psum.tile([P, ROWS], F32, tag="bank")
             mx_product(acc, mx["hidden"], lambda g: slice(g * ROWS + i * P, g * ROWS + (i + 1) * P), mx[n])
-            z = score_pool.tile([P, ROWS], F32, tag="score")
-            nc.vector.tensor_tensor(out=z[:], in0=acc[:], in1=baddr_all[:, c * ROWS : (c + 1) * ROWS], op=ALU.add)
-            scores[n, i] = z
+            if i == 0:
+                z = score_pool.tile([P, TILES, ROWS], F32, tag="score")
+                scores[n] = z
+            nc.vector.tensor_tensor(
+                out=scores[n][:, i, :], in0=acc[:], in1=baddr_all[:, c * ROWS : (c + 1) * ROWS], op=ALU.add
+            )
 
         def maximum(n, i):
             c = ORDER[n][1]
-            nc.vector.tensor_reduce(out=neg_max[:, i, c : c + 1], in_=scores[n, i][:], axis=AXIS.X, op=ALU.max, negate=True)
+            if i % MAX_WIDE == 0:
+                nc.vector.tensor_reduce(
+                    out=neg_max[:, i : i + MAX_WIDE, c], in_=scores[n][:, i : i + MAX_WIDE, :], axis=AXIS.X, op=ALU.max, negate=True
+                )
 
         def exponential(n, i):
             c = ORDER[n][1]
             nc.scalar.activation(
-                out=exp_scores[:, i, c * ROWS : (c + 1) * ROWS], in_=scores[n, i][:], func=ACT.Exp,
+                out=exp_scores[:, i, c * ROWS : (c + 1) * ROWS], in_=scores[n][:, i, :], func=ACT.Exp,
                 bias=neg_max[:, i, c : c + 1], scale=1.0, accum_out=exp_sum[:, i, c : c + 1],
             )
 
@@ -300,6 +317,8 @@ def tile_persistentgrucell_pc_kernel(
             nc.sync.dma_start(out=out[i * P : (i + 1) * P, cols], in_=result[:, i, cols])
 
         def load_later(n):
+            if n in (2, 4, 6):
+                load_memory(n // 2)
             if n + RAW_BUFS < len(blocks):
                 raw[n + RAW_BUFS] = load_rows(raw_pool, blocks[n + RAW_BUFS], 2)
 
@@ -334,7 +353,8 @@ def tile_persistentgrucell_pc_kernel(
             if n < count:
                 quantise(n, mx_pool, 0, TILES)
 
-        sum_hidden(0, half)
+        for i in range(TILES):
+            sum_hidden(i, i + 1)
         transpose_tiles("hidden", hidden_raw, (0, 1))
         transpose_tiles("hidden", hidden_raw, (2, 3))
         quantise("hidden", const, 0, TILES)
@@ -352,10 +372,10 @@ def tile_persistentgrucell_pc_kernel(
 
         begin_and_finish(0)
         spread_gate_biases()
-        sum_hidden(half, TILES)
-        if is_addr(0):
-            spread_baddr()
-            begin_and_finish(1)
+        spread_baddr()
+        line_up(2)
+        begin_and_finish(1)
+        line_up(3)
         left = {}
         ready = []
         exps = []
@@ -363,10 +383,6 @@ def tile_persistentgrucell_pc_kernel(
             kind, c = ORDER[n]
             for i in range(TILES):
                 product(n, i)
-            if n == 0 and not is_addr(0):
-                start_block(1)
-                finish_block(1)
-                spread_baddr()
             start_block(n + 2)
             if is_addr(n):
                 for i in range(TILES):
@@ -382,8 +398,6 @@ def tile_persistentgrucell_pc_kernel(
                 if m == last_addr:
                     totals[2]()
             if not is_addr(n):
-                if kind == FORGET:
-                    halve_memory(c)
                 banks = turn_back(n)
                 for i in range(TILES):
                     multiply(n, i, banks[i])

@@ -99,10 +99,10 @@ def tile_persistentgrucell_pc_kernel(
                 )
 
         for n in range(1, 4):
-            raw[n] = load_rows(raw_pool, blocks[n], 2)
+            raw[n] = load_rows(raw_pool, blocks[n], 1)
         load_memory(0)
         for n in range(4, RAW_BUFS):
-            raw[n] = load_rows(raw_pool, blocks[n], 2)
+            raw[n] = load_rows(raw_pool, blocks[n], 1)
 
         gate_bias = const.tile([P, 2 * SLOT_TILES], F32)
         baddr_all = const.tile([P, SLOTS], BF16)
@@ -320,7 +320,7 @@ def tile_persistentgrucell_pc_kernel(
             if n in (2, 4, 6):
                 load_memory(n // 2)
             if n + RAW_BUFS < len(blocks):
-                raw[n + RAW_BUFS] = load_rows(raw_pool, blocks[n + RAW_BUFS], 2)
+                raw[n + RAW_BUFS] = load_rows(raw_pool, blocks[n + RAW_BUFS], 1)
 
         half = TILES // 2
         hidden_rows = hidden_raw[:].rearrange("p (i k) -> p i k", i=TILES)

@@ -90,17 +90,9 @@ def tile_persistentgrucell_pc_kernel(
         half_memory = const.tile([P, TILES, SLOTS], BF16)
         memory = persistent_memory.rearrange("(i p) n -> p i n", p=P)
 
-        def load_memory(c):
-            cols = slice(c * ROWS, (c + 1) * ROWS)
-            nc.sync.dma_start(out=half_memory[:, :, cols], in_=memory[:, :, cols])
-            for i in range(TILES):
-                nc.gpsimd.tensor_scalar(
-                    out=half_memory[:, i, cols], in0=half_memory[:, i, cols], scalar1=0.5, scalar2=0.0, op0=ALU.mult, op1=ALU.add
-                )
-
         for n in range(1, 4):
             raw[n] = load_rows(raw_pool, blocks[n], 1)
-        load_memory(0)
+        nc.sync.dma_start(out=half_memory[:], in_=memory)
         for n in range(4, RAW_BUFS):
             raw[n] = load_rows(raw_pool, blocks[n], 1)
 
@@ -317,8 +309,6 @@ def tile_persistentgrucell_pc_kernel(
             nc.sync.dma_start(out=out[i * P : (i + 1) * P, cols], in_=result[:, i, cols])
 
         def load_later(n):
-            if n in (2, 4, 6):
-                load_memory(n // 2)
             if n + RAW_BUFS < len(blocks):
                 raw[n + RAW_BUFS] = load_rows(raw_pool, blocks[n + RAW_BUFS], 1)
 
@@ -398,6 +388,11 @@ def tile_persistentgrucell_pc_kernel(
                 if m == last_addr:
                     totals[2]()
             if not is_addr(n):
+                if kind == FORGET:
+                    cols = slice(c * ROWS, (c + 1) * ROWS)
+                    nc.vector.tensor_scalar(
+                        out=half_memory[:, :, cols], in0=half_memory[:, :, cols], scalar1=0.5, scalar2=None, op0=ALU.mult
+                    )
                 banks = turn_back(n)
                 for i in range(TILES):
                     multiply(n, i, banks[i])

@@ -35,7 +35,7 @@ ORDER = (
 
 SCALED = {(1, 0), (2, 0), (3, 0)}
 ON_GPSIMD = SCALED
-MAX_WIDE = 4
+MAX_WIDE = 2
 PERMUTE = "------------"
 GP_ADDS = "1111111111111010"
 FLOPS = 2 * BATCH * HIDDEN * SLOTS * 3
@@ -366,6 +366,12 @@ def tile_persistentgrucell_pc_kernel(
         line_up(2)
         begin_and_finish(1)
         line_up(3)
+        def halve(c):
+            cols = slice(c * ROWS, (c + 1) * ROWS)
+            nc.vector.tensor_scalar(
+                out=half_memory[:, :, cols], in0=half_memory[:, :, cols], scalar1=0.5, scalar2=None, op0=ALU.mult
+            )
+
         left = {}
         ready = []
         exps = []
@@ -377,6 +383,8 @@ def tile_persistentgrucell_pc_kernel(
             if is_addr(n):
                 for i in range(TILES):
                     maximum(n, i)
+                if n:
+                    halve(c)
                 exps.append(n)
                 if kind == ADDR and n == last_addr:
                     totals[0]()
@@ -387,12 +395,9 @@ def tile_persistentgrucell_pc_kernel(
                     exponential(m, i)
                 if m == last_addr:
                     totals[2]()
+            if n == 1:
+                halve(0)
             if not is_addr(n):
-                if kind == FORGET:
-                    cols = slice(c * ROWS, (c + 1) * ROWS)
-                    nc.vector.tensor_scalar(
-                        out=half_memory[:, :, cols], in0=half_memory[:, :, cols], scalar1=0.5, scalar2=None, op0=ALU.mult
-                    )
                 banks = turn_back(n)
                 for i in range(TILES):
                     multiply(n, i, banks[i])

from contextlib import ExitStack

import concourse.mybir as mybir
from concourse.masks import make_identity

F32 = mybir.dt.float32
BF16 = mybir.dt.bfloat16
U32 = mybir.dt.uint32
U8 = mybir.dt.uint8
FP8X4 = mybir.dt.float8_e4m3fn_x4
ALU = mybir.AluOpType
ACT = mybir.ActivationFunctionType
AXIS = mybir.AxisListType

P = 128
BATCH = 512
HIDDEN = 1024
SLOTS = 2048
PACK = 4
PASSES = HIDDEN // (P * PACK)
PAIRS = 2
ROWS = 512
TILES = ROWS // P
ROW_WORDS = HIDDEN // 2
CHUNKS = SLOTS // ROWS
SLOT_TILES = SLOTS // P
RAW_BUFS = 5
AHEAD = 2
ADDR = 0
FORGET = 1
WRITE = 2
ORDER = (
    (ADDR, 0), (FORGET, 0), (ADDR, 1), (FORGET, 1), (ADDR, 2), (FORGET, 2), (ADDR, 3), (FORGET, 3), (WRITE, 0), (WRITE, 1), (WRITE, 2), (WRITE, 3),
)

SCALED = {(1, 0), (2, 0), (3, 0)}
ON_GPSIMD = SCALED
MAX_WIDE = 2
PERMUTE = "------------"
GP_ADDS = "1111111111111010"
FLOPS = 2 * BATCH * HIDDEN * SLOTS * 3


def tile_persistentgrucell_pc_kernel(
    tc, hidden_new, persistent_memory, Waddr, baddr, Wwrite, bwrite, Wforget, bforget, out
):
    nc = tc.nc
    with ExitStack() as stack:
        stack.enter_context(tc.manual_schedule())
        const = stack.enter_context(tc.tile_pool(name="const", bufs=1))
        raw_pool = stack.enter_context(tc.tile_pool(name="raw", bufs=RAW_BUFS))
        grouped_pool = stack.enter_context(tc.tile_pool(name="grouped", bufs=2))
        mx_pool = stack.enter_context(tc.tile_pool(name="mx", bufs=4))
        lined_pool = stack.enter_context(tc.tile_pool(name="lined", bufs=2))
        score_pool = stack.enter_context(tc.tile_pool(name="score", bufs=2))
        gate_pool = stack.enter_context(tc.tile_pool(name="gate", bufs=2))
        psum = stack.enter_context(tc.psum_pool(name="psum", bufs=8))

        weights = {ADDR: Waddr, FORGET: Wforget, WRITE: Wwrite}
        blocks = [weights[kind][c * ROWS : (c + 1) * ROWS, :] for kind, c in ORDER]

        def load_rows(pool, rows, pieces):
            raw_rows = pool.tile([P, TILES * HIDDEN], BF16, tag="raw")
            tiles = raw_rows[:].rearrange("p (j k) -> p j k", j=TILES)
            source = rows.rearrange("(j p) k -> p j k", p=P)
            step = TILES // pieces
            for j in range(0, TILES, step):
                nc.sync.dma_start(out=tiles[:, j : j + step, :], in_=source[:, j : j + step, :])
            return raw_rows

        ident = const.tile([P, P], F32)
        make_identity(nc, ident[:])
        ident_bf16 = const.tile([P, P], BF16)
        make_identity(nc, ident_bf16[:])
        ones = const.tile([P, P], BF16)
        bias_rows = const.tile([P, P], BF16)
        nc.vector.memset(bias_rows[:], 0.0)
        baddr_row = const.tile([P, SLOTS], BF16)
        nc.vector.memset(baddr_row[:], 0.0)
        nc.vector.memset(ones[:], 1.0)

        hidden_raw = load_rows(const, hidden_new, 2)
        raw = {0: load_rows(raw_pool, blocks[0], 2)}
        for gate, bias in ((0, bforget), (1, bwrite)):
            nc.sync.dma_start(
                out=bias_rows[gate * SLOT_TILES : (gate + 1) * SLOT_TILES, :],
                in_=bias.rearrange("(t p) -> t p", p=P),
            )
        nc.sync.dma_start(out=baddr_row[0:1, :], in_=baddr.rearrange("(o n) -> o n", o=1))
        half_memory = const.tile([P, TILES, SLOTS], BF16)
        memory = persistent_memory.rearrange("(i p) n -> p i n", p=P)

        for n in range(1, 4):
            raw[n] = load_rows(raw_pool, blocks[n], 1)
        nc.sync.dma_start(out=half_memory[:], in_=memory)
        for n in range(4, RAW_BUFS):
            raw[n] = load_rows(raw_pool, blocks[n], 1)

        gate_bias = const.tile([P, 2 * SLOT_TILES], F32)
        baddr_all = const.tile([P, SLOTS], BF16)

        def spread_gate_biases():
            bias_bank = psum.tile([P, P], BF16, tag="bank")
            nc.tensor.transpose(bias_bank[:], bias_rows[:], ident_bf16[:])
            nc.scalar.mul(out=gate_bias[:], in_=bias_bank[:, 0 : 2 * SLOT_TILES], mul=0.5)

        def spread_baddr():
            for c in range(CHUNKS):
                cols = slice(c * ROWS, (c + 1) * ROWS)
                baddr_bank = psum.tile([P, ROWS], F32, tag="bank")
                nc.tensor.matmul(out=baddr_bank[:], lhsT=ones[:], rhs=baddr_row[:, cols], start=True, stop=True)
                nc.scalar.copy(out=baddr_all[:, cols], in_=baddr_bank[:])

        grouped = {}
        mx = {}
        lined = {}

        def line_up(n):
            if n >= len(blocks) or PERMUTE[n] == "-":
                return
            lined_rows = lined_pool.tile([P, TILES * HIDDEN], BF16, tag="lined")
            lined[n] = lined_rows
            source = raw[n][:].bitcast(F32).rearrange("p (b u i) -> p u b i", u=PAIRS, i=8)
            target = lined[n][:].bitcast(F32).rearrange("p (u b i) -> p u b i", u=PAIRS, i=8)
            if PERMUTE[n] == "V":
                nc.vector.tensor_copy(out=target, in_=source)
            else:
                nc.scalar.copy(out=target, in_=source)
            load_later(n)

        def stationary(n):
            return n != "hidden" and ORDER[n][0] != ADDR

        def grouped_view(n, j):
            words = grouped[n][:].bitcast(F32)
            if stationary(n):
                return words.rearrange("p (j g r u) -> p j g r u", j=TILES, g=PASSES, u=PAIRS)[:, j]
            return words.rearrange("p (g j r u) -> p j g r u", j=TILES, g=PASSES, u=PAIRS)[:, j]

        def transpose_tiles(n, raw_rows, tiles):
            words = lined[n][:].bitcast(F32) if n in lined else raw_rows[:].bitcast(F32)
            if n not in grouped:
                grouped_rows = grouped_pool.tile([P, PASSES * ROWS * PACK], BF16, tag="grouped", align_bytes=64)
                grouped[n] = grouped_rows
            banks = []
            for j in tiles:
                bank = psum.tile([P, PASSES, PAIRS, P], F32, tag="bank")
                for g in range(PASSES):
                    for u in range(PAIRS):
                        if n in lined:
                            first = ((u * TILES + j) * PASSES + g) * P
                            columns = slice(first, first + P)
                        else:
                            first = j * ROW_WORDS + g * PAIRS * P + u
                            columns = slice(first, j * ROW_WORDS + (g + 1) * PAIRS * P, PAIRS)
                        nc.tensor.transpose(bank[:, g, u, :], words[:, columns], ident[:])
                banks.append(bank)
            for j, bank in zip(tiles, banks):
                nc.scalar.copy(out=grouped_view(n, j), in_=bank[:].rearrange("p g u r -> p g r u"))

        def quantise(n, pool, first, last):
            if n not in mx:
                new_codes = pool.tile([P, PASSES * ROWS], U32, tag="codes", align_bytes=64)
                new_scales = pool.tile([P, PASSES * ROWS], U8, tag="scales", align_bytes=64)
                mx[n] = (new_codes, new_scales)
            codes, scales = mx[n]
            a, b = first * PASSES * P, last * PASSES * P
            nc.vector.quantize_mx(
                out=codes[:, a:b].bitcast(FP8X4), scales=scales[:, a:b], in_=grouped[n][:, a * PACK : b * PACK]
            )

        def mx_product(acc, still, still_cols, moving):
            for g in range(PASSES):
                s_cols = still_cols(g)
                m_cols = slice(g * ROWS, (g + 1) * ROWS)
                nc.tensor.matmul_mx(
                    out=acc[:],
                    lhsT=still[0][:, s_cols].bitcast(FP8X4),
                    lhsT_scale=still[1][:, s_cols],
                    rhs=moving[0][:, m_cols].bitcast(FP8X4),
                    rhs_scale=moving[1][:, m_cols],
                    start=(g == 0),
                    stop=(g == PASSES - 1),
                )

        exp_scores = const.tile([P, TILES, SLOTS], F32)
        neg_max = const.tile([P, TILES, CHUNKS], F32)
        exp_sum = const.tile([P, TILES, CHUNKS], F32)
        result = const.tile([P, TILES, SLOTS], F32)
        scores = {}
        gates = {}

        def score(n, i):
            c = ORDER[n][1]
            acc = psum.tile([P, ROWS], F32, tag="bank")
            mx_product(acc, mx["hidden"], lambda g: slice(g * ROWS + i * P, g * ROWS + (i + 1) * P), mx[n])
            if i == 0:
                z = score_pool.tile([P, TILES, ROWS], F32, tag="score")
                scores[n] = z
            nc.vector.tensor_tensor(
                out=scores[n][:, i, :], in0=acc[:], in1=baddr_all[:, c * ROWS : (c + 1) * ROWS], op=ALU.add
            )

        def maximum(n, i):
            c = ORDER[n][1]
            if i % MAX_WIDE == 0:
                nc.vector.tensor_reduce(
                    out=neg_max[:, i : i + MAX_WIDE, c], in_=scores[n][:, i : i + MAX_WIDE, :], axis=AXIS.X, op=ALU.max, negate=True
                )

        def exponential(n, i):
            c = ORDER[n][1]
            nc.scalar.activation(
                out=exp_scores[:, i, c * ROWS : (c + 1) * ROWS], in_=scores[n][:, i, :], func=ACT.Exp,
                bias=neg_max[:, i, c : c + 1], scale=1.0, accum_out=exp_sum[:, i, c : c + 1],
            )

        def gate(n, j):
            kind, c = ORDER[n]
            acc = psum.tile([P, BATCH], F32, tag="bank")
            mx_product(acc, mx[n], lambda g: slice((j * PASSES + g) * P, (j * PASSES + g + 1) * P), mx["hidden"])
            if n not in gates:
                gate_t = gate_pool.tile([P, TILES, BATCH], F32, tag="gate")
                gates[n] = gate_t
            t = (kind - FORGET) * SLOT_TILES + c * TILES + j
            nc.scalar.activation(
                out=gates[n][:, j, :],
                in_=acc[:],
                func=ACT.Tanh,
                bias=gate_bias[:, t : t + 1],
                scale=0.5,
            )

        def product(n, i):
            if ORDER[n][0] == ADDR:
                score(n, i)
            else:
                gate(n, i)

        def turn_back(n):
            kind, c = ORDER[n]
            cols = slice(c * ROWS, (c + 1) * ROWS)
            banks = []
            for i in range(TILES):
                bank = psum.tile([P, ROWS], F32, tag="bank")
                for j in range(TILES):
                    nc.tensor.transpose(bank[:, j * P : (j + 1) * P], gates[n][:, j, i * P : (i + 1) * P], ident[:])
                banks.append(bank)
            return banks

        def multiply(n, i, bank):
            kind, c = ORDER[n]
            cols = slice(c * ROWS, (c + 1) * ROWS)
            if kind == FORGET:
                nc.vector.scalar_tensor_tensor(
                    out=result[:, i, cols], in0=bank[:], scalar=1.0, in1=half_memory[:, i, cols], op0=ALU.add, op1=ALU.mult
                )
            else:
                nc.vector.scalar_tensor_tensor(
                    out=exp_scores[:, i, cols], in0=bank[:], scalar=1.0, in1=exp_scores[:, i, cols], op0=ALU.add, op1=ALU.mult
                )

        small = [P, TILES, CHUNKS]
        chunk_scale = const.tile(small, F32)
        hidden_sum = const.tile([P, TILES], F32)
        neg_top = const.tile([P, TILES], F32)
        below_top = const.tile(small, F32)
        rescale = const.tile(small, F32)
        rescaled_sum = const.tile(small, F32)
        row_sum = const.tile([P, TILES], F32)
        inv_row_sum = const.tile([P, TILES], F32)
        row_scale = const.tile([P, TILES], F32)

        totals = [
            lambda: nc.vector.tensor_reduce(out=neg_top[:], in_=neg_max[:], axis=AXIS.X, op=ALU.min),
            lambda: nc.vector.tensor_tensor(
                out=below_top[:], in0=neg_top[:].unsqueeze(2).to_broadcast(small), in1=neg_max[:], op=ALU.subtract
            ),
            lambda: nc.scalar.activation(out=rescale[:], in_=below_top[:], func=ACT.Exp),
            lambda: nc.vector.tensor_tensor(out=rescaled_sum[:], in0=rescale[:], in1=exp_sum[:], op=ALU.mult),
            lambda: nc.vector.tensor_reduce(out=row_sum[:], in_=rescaled_sum[:], axis=AXIS.X, op=ALU.add),
            lambda: nc.vector.reciprocal(out=inv_row_sum[:], in_=row_sum[:]),
            lambda: nc.vector.scalar_tensor_tensor(
                out=row_scale[:], in0=hidden_sum[:], scalar=0.5 / HIDDEN, in1=inv_row_sum[:], op0=ALU.mult, op1=ALU.mult
            ),
            lambda: nc.vector.tensor_tensor(
                out=chunk_scale[:], in0=rescale[:], in1=row_scale[:].unsqueeze(2).to_broadcast(small), op=ALU.mult
            ),
        ]

        def scale_scores(c):
            for i in range(TILES):
                if (c, i) in SCALED:
                    cols = slice(c * ROWS, (c + 1) * ROWS)
                    nc.scalar.mul(out=exp_scores[:, i, cols], in_=exp_scores[:, i, cols], mul=chunk_scale[:, i, c : c + 1])

        def finish(c, i):
            cols = slice(c * ROWS, (c + 1) * ROWS)
            if (c, i) in SCALED:
                adder = nc.gpsimd if (c, i) in ON_GPSIMD else nc.vector
                adder.tensor_tensor(
                    out=result[:, i, cols], in0=exp_scores[:, i, cols], in1=result[:, i, cols], op=ALU.add
                )
            else:
                nc.vector.scalar_tensor_tensor(
                    out=result[:, i, cols], in0=exp_scores[:, i, cols], scalar=chunk_scale[:, i, c : c + 1],
                    in1=result[:, i, cols], op0=ALU.mult, op1=ALU.add,
                )
            nc.sync.dma_start(out=out[i * P : (i + 1) * P, cols], in_=result[:, i, cols])

        def load_later(n):
            if n + RAW_BUFS < len(blocks):
                raw[n + RAW_BUFS] = load_rows(raw_pool, blocks[n + RAW_BUFS], 1)

        half = TILES // 2
        hidden_rows = hidden_raw[:].rearrange("p (i k) -> p i k", i=TILES)

        def sum_hidden(first, last):
            nc.vector.tensor_reduce(
                out=hidden_sum[:, first:last], in_=hidden_rows[:, first:last, :], axis=AXIS.X, op=ALU.add
            )

        def halve_memory(c):
            cols = slice(c * ROWS, (c + 1) * ROWS)
            nc.vector.tensor_scalar(
                out=half_memory[:, :, cols], in0=half_memory[:, :, cols], scalar1=0.5, scalar2=None, op0=ALU.mult
            )

        count = len(ORDER)
        last_addr = max(n for n in range(count) if ORDER[n][0] == ADDR)

        def is_addr(n):
            return 0 <= n < count and ORDER[n][0] == ADDR

        def start_block(n):
            if n < count:
                transpose_tiles(n, raw[n], (0, 1))
                transpose_tiles(n, raw[n], (2, 3))
                if n not in lined:
                    load_later(n)

        def finish_block(n):
            if n < count:
                quantise(n, mx_pool, 0, TILES)

        for i in range(TILES):
            sum_hidden(i, i + 1)
        transpose_tiles("hidden", hidden_raw, (0, 1))
        transpose_tiles("hidden", hidden_raw, (2, 3))
        quantise("hidden", const, 0, TILES)

        def begin_and_finish(n):
            if n < count and stationary(n):
                transpose_tiles(n, raw[n], (0, 1))
                quantise(n, mx_pool, 0, half)
                transpose_tiles(n, raw[n], (2, 3))
                quantise(n, mx_pool, half, TILES)
                load_later(n)
            else:
                start_block(n)
                finish_block(n)

        begin_and_finish(0)
        spread_gate_biases()
        spread_baddr()
        line_up(2)
        begin_and_finish(1)
        line_up(3)
        def halve(c):
            cols = slice(c * ROWS, (c + 1) * ROWS)
            nc.vector.tensor_scalar(
                out=half_memory[:, :, cols], in0=half_memory[:, :, cols], scalar1=0.5, scalar2=None, op0=ALU.mult
            )

        left = {}
        ready = []
        exps = []
        for n in range(count):
            kind, c = ORDER[n]
            for i in range(TILES):
                product(n, i)
            start_block(n + 2)
            if is_addr(n):
                for i in range(TILES):
                    maximum(n, i)
                if n:
                    halve(c)
                exps.append(n)
                if kind == ADDR and n == last_addr:
                    totals[0]()
                    totals[1]()
            if (not is_addr(n) or n + 1 < count and is_addr(n + 1)) and exps and exps[0] < n:
                m = exps.pop(0)
                for i in range(TILES):
                    exponential(m, i)
                if m == last_addr:
                    totals[2]()
            if n == 1:
                halve(0)
            if not is_addr(n):
                banks = turn_back(n)
                for i in range(TILES):
                    multiply(n, i, banks[i])
                left[c] = left.get(c, 0) + 1
                if left[c] == 2:
                    ready.append(c)
            finish_block(n + 2)
            if n == last_addr + 1:
                for step in totals[3:]:
                    step()
            if n > last_addr and n + 1 < count and ORDER[n + 1][0] == WRITE:
                scale_scores(ORDER[n + 1][1])
            if n > last_addr:
                for k in range(1 if n + 1 < count else len(ready)):
                    if ready:
                        c = ready.pop(0)
                        for i in range(TILES):
                            finish(c, i)
